import numpy as np
import ml_dtypes


def mxq(x, axis, fmt="e4m3"):
    dtype, down = {"e4m3": (ml_dtypes.float8_e4m3fn, 7), "e5m2": (ml_dtypes.float8_e5m2, 14)}[fmt]
    v = np.moveaxis(np.asarray(x, np.float32).astype(ml_dtypes.bfloat16).astype(np.float64), axis, -1)
    blocks = v.reshape(v.shape[:-1] + (-1, 32))
    amax = np.abs(blocks).max(-1, keepdims=True)
    byte = np.maximum(np.where(amax > 0, np.frexp(amax)[1] - 1 + 127, 0) - down, 1)
    scale = np.exp2(byte - 127.0)
    codes = (blocks / scale).astype(np.float32).astype(dtype).astype(np.float64)
    return np.moveaxis((codes * scale).reshape(v.shape), -1, axis)


WIDE = False


def mx_kscale(k):
    if not WIDE:
        return np.ones(k)
    levels = np.array([10, -10, 5, -5, 0])
    a = np.random.permutation(np.resize(levels, k // 512 * 4)).reshape(k // 512, 4)
    idx = np.arange(k)
    return np.exp2(a[idx // 512, idx % 128 // 32])


BF16 = ml_dtypes.bfloat16


def bf(x):
    return np.asarray(x, np.float32).astype(BF16)


def f64(x):
    return np.asarray(x).astype(np.float64)


E2M1 = np.array([0.0, 0.5, 1.0, 1.5, 2.0, 3.0, 4.0, 6.0, -0.0, -0.5, -1.0, -1.5, -2.0, -3.0, -4.0, -6.0])


def pack_weight(w, fmt):
    k, n = w.shape
    w = f64(bf(w)).reshape(k // 32, 32, n)
    amax = np.abs(w).max(1)
    if fmt == "e4m3":
        byte = np.frexp(amax)[1] - 1 + 127 - 7
    else:
        mant, ex = np.frexp(amax / 6.0)
        byte = np.where(mant > 0.5, ex, ex - 1) + 127
    byte = np.clip(np.where(amax > 0, byte, 1), 1, 254)
    scaled = (w * np.exp2(127.0 - byte)[:, None, :]).reshape(k, n).astype(np.float32)
    by_word = np.ascontiguousarray(scaled.reshape(k // 512, 128, 4, n).transpose(0, 1, 3, 2))
    if fmt == "e4m3":
        words = by_word.astype(ml_dtypes.float8_e4m3fn).view(np.uint8)
    else:
        c = by_word.astype(ml_dtypes.float4_e2m1fn).view(np.uint8) & 0xF
        words = c[..., 0::2] | (c[..., 1::2] << 4)
    return np.ascontiguousarray(words), np.ascontiguousarray(byte.astype(np.uint8).reshape(k // 512, 16, n))


def unpack_weight(words, scales, fmt):
    g, p, n, _ = words.shape
    if fmt == "e4m3":
        vals = np.ascontiguousarray(words).view(ml_dtypes.float8_e4m3fn).astype(np.float64)
    else:
        nib = np.empty((g, p, n, 4), np.uint8)
        nib[..., 0::2] = words & 0xF
        nib[..., 1::2] = words >> 4
        vals = E2M1[nib]
    vals = vals * np.repeat(np.exp2(scales.astype(np.float64) - 127.0), 8, axis=1)[..., None]
    return vals.transpose(0, 1, 3, 2).reshape(g * 512, n)


B, Nb1, Nw1, Nb2x, Nb2y, Nw2x, Nw2y, R, C = 4096, 2, 16, 4, 4, 16, 16, 16, 2
J1 = Nb1 * Nb1
K1 = C * Nw1 * Nw1
J3 = Nb2x * Nb2y
L1 = J3 * R
J2 = J3 * J1


def setup_inputs():
    s = mx_kscale(K1)
    sx = s.reshape(Nw1, Nw1, C)[:, None, :, :]
    x = np.random.standard_normal((B, Nb1, Nw1, Nb1, Nw1, C)) * sx
    k1 = np.random.standard_normal((J1, K1, L1)) / np.sqrt(K1) / s[None, :, None]
    k1_words, k1_scales = pack_weight(k1.reshape(-1, L1), "e4m3")
    return {"x": bf(x.reshape(B, Nb1 * Nw1 * Nb1 * Nw1, C)),
            "k1_words": k1_words,
            "k1_scales": k1_scales,
            "b1": bf(np.random.standard_normal((1, J1, L1)) * 0.3)}


def reference(x, k1_words, k1_scales, b1):
    h = f64(x).reshape(B, Nb1, Nw1, Nb1, Nw1, C).transpose(0, 1, 3, 2, 4, 5).reshape(B, J1, K1)
    hq = mxq(h, 2, "e4m3").transpose(1, 0, 2)
    k1 = unpack_weight(k1_words, k1_scales, "e4m3").reshape(J1, K1, L1)
    y = (hq @ k1).transpose(1, 0, 2) + f64(b1)
    y = y.reshape(B, J1, J3, R).transpose(0, 3, 1, 2)
    return y.reshape(B, J2, R)

@@ -1,0 +1,170 @@
+from contextlib import ExitStack
+
+import concourse.mybir as mybir
+from concourse.masks import make_identity
+
+F32 = mybir.dt.float32
+BF16 = mybir.dt.bfloat16
+I32 = mybir.dt.int32
+U32 = mybir.dt.uint32
+U8 = mybir.dt.uint8
+FP8X4 = mybir.dt.float8_e4m3fn_x4
+
+P = 128
+SAMPLES = 4096
+BLOCKS = 4
+K = 512
+L = 256
+R = 16
+M = 16
+WORDS = 1024
+K_WORDS = K // 2
+
+TILES = SAMPLES // P
+TILES_PER_CHUNK = 2
+CHUNKS = TILES // TILES_PER_CHUNK
+LOADS_AHEAD = 3
+
+FLOPS = 2 * SAMPLES * BLOCKS * K * L
+
+
+def tile_switchnet_fstar_pa_t_e_kernel(tc, x, k1_words, k1_scales, b1, out):
+    nc = tc.nc
+    x_chunks = x.rearrange("(c p s) g ch -> c p (s g ch)", p=P, s=TILES_PER_CHUNK)
+    out_chunks = out.rearrange("(c p s) q r -> c p (s q r)", p=P, s=TILES_PER_CHUNK)
+
+    with ExitStack() as stack:
+        consts = stack.enter_context(tc.tile_pool(name="consts", bufs=1))
+        x_pool = stack.enter_context(tc.tile_pool(name="x", bufs=LOADS_AHEAD + 1))
+        sorted_pool = stack.enter_context(tc.tile_pool(name="sorted", bufs=3))
+        grouped_pool = stack.enter_context(tc.tile_pool(name="grouped", bufs=3))
+        codes_pool = stack.enter_context(tc.tile_pool(name="codes", bufs=3))
+        y_pool = stack.enter_context(tc.tile_pool(name="y", bufs=3))
+        flipped_pool = stack.enter_context(tc.psum_pool(name="flipped", bufs=4))
+        acc_pool = stack.enter_context(tc.psum_pool(name="acc", bufs=4))
+        stack.enter_context(tc.manual_schedule())
+
+        x_tiles = {}
+        sorted_tiles = {}
+        grouped_tiles = {}
+        codes_tiles = {}
+        acc_tiles = {}
+        y_tiles = {}
+
+        def load(c):
+            x_sb = x_pool.tile([P, TILES_PER_CHUNK, 2 * WORDS], BF16)
+            nc.sync.dma_start(out=x_sb[:].rearrange("p s e -> p (s e)"), in_=x_chunks[c])
+            x_tiles[c] = x_sb
+
+        w_scales = consts.tile([P, BLOCKS, L], U8, align_bytes=64)
+        nc.vector.memset(w_scales[:].rearrange("p j l -> p (j l)").bitcast(I32), 0)
+        load(0)
+        w_words = consts.tile([P, BLOCKS, L], U32, align_bytes=64)
+        nc.sync.dma_start(
+            out=w_words[:].bitcast(I32),
+            in_=k1_words.rearrange("j p l t -> p j (l t)").bitcast(I32),
+        )
+        for quadrant in range(4):
+            nc.sync.dma_start(
+                out=w_scales[32 * quadrant : 32 * quadrant + 4].bitcast(I32),
+                in_=k1_scales[:, 4 * quadrant : 4 * quadrant + 4, :].rearrange("j q l -> q j l").bitcast(I32),
+            )
+        for c in range(1, LOADS_AHEAD):
+            load(c)
+
+        identity = consts.tile([P, P], F32)
+        make_identity(nc, identity[:])
+
+        bias_bf16 = consts.tile([P, BLOCKS * L], BF16)
+        nc.scalar.dma_start(out=bias_bf16[:], in_=b1.rearrange("o j l -> (o j l)").partition_broadcast(P))
+        bias = consts.tile([P, R, BLOCKS, M], F32)
+        nc.gpsimd.tensor_copy(
+            out=bias[:], in_=bias_bf16[:].rearrange("p (j m r) -> p r j m", j=BLOCKS, m=M, r=R)
+        )
+
+        def sort_words(i):
+            c, s = divmod(i, TILES_PER_CHUNK)
+            words = x_tiles[c][:, s, :].bitcast(F32)
+            words = words.rearrange("p (br wr bc a u) -> p br bc u wr a", br=2, wr=16, bc=2, a=8, u=2)
+            sorted_sb = sorted_pool.tile([P, BLOCKS, 2, P], F32)
+            for j in range(BLOCKS):
+                copy = nc.vector.tensor_copy if j == BLOCKS - 1 else nc.scalar.copy
+                copy(
+                    out=sorted_sb[:, j].rearrange("p u (wr a) -> p u wr a", a=8),
+                    in_=words[:, j // 2, j % 2],
+                )
+            sorted_tiles[i] = sorted_sb
+
+        def transpose_words(i):
+            sorted_sb = sorted_tiles[i]
+            grouped = grouped_pool.tile([P, BLOCKS, P, 4], BF16, align_bytes=64)
+            for br in range(2):
+                flipped = flipped_pool.tile([P, 2, 2, P], F32)
+                for bc in range(2):
+                    for u in range(2):
+                        nc.tensor.transpose(flipped[:, bc, u, :], sorted_sb[:, 2 * br + bc, u, :], identity[:])
+                nc.scalar.copy(
+                    out=grouped[:, 2 * br : 2 * br + 2].bitcast(F32),
+                    in_=flipped[:].rearrange("p bc u b -> p bc b u"),
+                )
+            grouped_tiles[i] = grouped
+
+        def quantise(i):
+            grouped = grouped_tiles[i]
+            codes = codes_pool.tile([P, BLOCKS, P], U32, align_bytes=64)
+            scales = codes_pool.tile([P, BLOCKS, P], U8, align_bytes=64)
+            nc.vector.quantize_mx(
+                out=codes[:].rearrange("p j b -> p (j b)").bitcast(FP8X4),
+                scales=scales[:].rearrange("p j b -> p (j b)"),
+                in_=grouped[:].rearrange("p j b t -> p (j b t)"),
+            )
+            codes_tiles[i] = (codes, scales)
+
+        def multiply(i):
+            codes, scales = codes_tiles[i]
+            banks = []
+            for br in range(2):
+                acc = acc_pool.tile([P, 2, L], F32)
+                for bc in range(2):
+                    j = 2 * br + bc
+                    nc.tensor.matmul_mx(
+                        out=acc[:, bc, :],
+                        lhsT=codes[:, j, :].bitcast(FP8X4),
+                        lhsT_scale=scales[:, j, :],
+                        rhs=w_words[:, j, :].bitcast(FP8X4),
+                        rhs_scale=w_scales[:, j, :],
+                        start=True,
+                        stop=True,
+                    )
+                banks.append(acc)
+            acc_tiles[i] = banks
+
+        def add_bias(i):
+            c, s = divmod(i, TILES_PER_CHUNK)
+            if s == 0:
+                y_new = y_pool.tile([P, TILES_PER_CHUNK, R, BLOCKS, M], F32)
+                y_tiles[c] = y_new
+            y_sb = y_tiles[c]
+            for br, acc in enumerate(acc_tiles[i]):
+                nc.vector.tensor_tensor(
+                    out=y_sb[:, s, :, 2 * br : 2 * br + 2, :],
+                    in0=acc[:].rearrange("p bc (m r) -> p r bc m", m=M, r=R),
+                    in1=bias[:, :, 2 * br : 2 * br + 2, :],
+                    op=mybir.AluOpType.add,
+                )
+            if s == TILES_PER_CHUNK - 1:
+                nc.sync.dma_start(out=out_chunks[c], in_=y_sb[:].rearrange("p s r j m -> p (s r j m)"))
+
+        for t in range(TILES + 3):
+            if t % TILES_PER_CHUNK == 0 and t // TILES_PER_CHUNK + LOADS_AHEAD < CHUNKS:
+                load(t // TILES_PER_CHUNK + LOADS_AHEAD)
+            if 0 <= t - 2 < TILES:
+                quantise(t - 2)
+            if t < TILES:
+                sort_words(t)
+            if 0 <= t - 1 < TILES:
+                transpose_words(t - 1)
+            if 0 <= t - 2 < TILES:
+                multiply(t - 2)
+            if 0 <= t - 3 < TILES:
+                add_bias(t - 3)

@@ -23,15 +23,15 @@ K_WORDS = K // 2
 TILES = SAMPLES // P
 TILES_PER_CHUNK = 2
 CHUNKS = TILES // TILES_PER_CHUNK
-LOADS_AHEAD = 3
+LOADS_AHEAD = 6
 
 FLOPS = 2 * SAMPLES * BLOCKS * K * L
 
 
 def tile_switchnet_fstar_pa_t_e_kernel(tc, x, k1_words, k1_scales, b1, out):
     nc = tc.nc
-    x_chunks = x.rearrange("(c p s) g ch -> c p (s g ch)", p=P, s=TILES_PER_CHUNK)
-    out_chunks = out.rearrange("(c p s) q r -> c p (s q r)", p=P, s=TILES_PER_CHUNK)
+    x_chunks = x.rearrange("(c p s) g ch -> c p s (g ch)", p=P, s=TILES_PER_CHUNK)
+    out_chunks = out.rearrange("(c p s) q r -> c p s (q r)", p=P, s=TILES_PER_CHUNK)
 
     with ExitStack() as stack:
         consts = stack.enter_context(tc.tile_pool(name="consts", bufs=1))
@@ -39,7 +39,7 @@ def tile_switchnet_fstar_pa_t_e_kernel(tc, x, k1_words, k1_scales, b1, out):
         sorted_pool = stack.enter_context(tc.tile_pool(name="sorted", bufs=3))
         grouped_pool = stack.enter_context(tc.tile_pool(name="grouped", bufs=3))
         codes_pool = stack.enter_context(tc.tile_pool(name="codes", bufs=3))
-        y_pool = stack.enter_context(tc.tile_pool(name="y", bufs=3))
+        y_pool = stack.enter_context(tc.tile_pool(name="y", bufs=4))
         flipped_pool = stack.enter_context(tc.psum_pool(name="flipped", bufs=4))
         acc_pool = stack.enter_context(tc.psum_pool(name="acc", bufs=4))
         stack.enter_context(tc.manual_schedule())
@@ -53,7 +53,11 @@ def tile_switchnet_fstar_pa_t_e_kernel(tc, x, k1_words, k1_scales, b1, out):
 
         def load(c):
             x_sb = x_pool.tile([P, TILES_PER_CHUNK, 2 * WORDS], BF16)
-            nc.sync.dma_start(out=x_sb[:].rearrange("p s e -> p (s e)"), in_=x_chunks[c])
+            if c == 0:
+                for s in range(TILES_PER_CHUNK):
+                    nc.sync.dma_start(out=x_sb[:, s, :], in_=x_chunks[c][:, s, :])
+            else:
+                nc.sync.dma_start(out=x_sb[:], in_=x_chunks[c])
             x_tiles[c] = x_sb
 
         w_scales = consts.tile([P, BLOCKS, L], U8, align_bytes=64)
@@ -75,24 +79,42 @@ def tile_switchnet_fstar_pa_t_e_kernel(tc, x, k1_words, k1_scales, b1, out):
         identity = consts.tile([P, P], F32)
         make_identity(nc, identity[:])
 
-        bias_bf16 = consts.tile([P, BLOCKS * L], BF16)
-        nc.scalar.dma_start(out=bias_bf16[:], in_=b1.rearrange("o j l -> (o j l)").partition_broadcast(P))
+        ones = consts.tile([P, P], BF16)
+        nc.vector.memset(ones[:], 1.0)
+        bias_row = consts.tile([P, BLOCKS, L], BF16)
+        nc.vector.memset(bias_row[:], 0.0)
+        nc.scalar.dma_start(out=bias_row[0:1], in_=b1)
         bias = consts.tile([P, R, BLOCKS, M], F32)
-        nc.gpsimd.tensor_copy(
-            out=bias[:], in_=bias_bf16[:].rearrange("p (j m r) -> p r j m", j=BLOCKS, m=M, r=R)
-        )
+
+        def spread_bias():
+            for br in range(2):
+                spread = acc_pool.tile([P, 2, L], F32, tag="acc")
+                nc.tensor.matmul(
+                    out=spread[:].rearrange("p bc l -> p (bc l)"),
+                    lhsT=ones[:],
+                    rhs=bias_row[:, 2 * br : 2 * br + 2, :].rearrange("p bc l -> p (bc l)"),
+                    start=True,
+                    stop=True,
+                )
+                nc.vector.tensor_copy(
+                    out=bias[:, :, 2 * br : 2 * br + 2, :],
+                    in_=spread[:].rearrange("p bc (m r) -> p r bc m", m=M, r=R),
+                )
 
         def sort_words(i):
             c, s = divmod(i, TILES_PER_CHUNK)
             words = x_tiles[c][:, s, :].bitcast(F32)
             words = words.rearrange("p (br wr bc a u) -> p br bc u wr a", br=2, wr=16, bc=2, a=8, u=2)
             sorted_sb = sorted_pool.tile([P, BLOCKS, 2, P], F32)
-            for j in range(BLOCKS):
-                copy = nc.vector.tensor_copy if j == BLOCKS - 1 else nc.scalar.copy
-                copy(
-                    out=sorted_sb[:, j].rearrange("p u (wr a) -> p u wr a", a=8),
-                    in_=words[:, j // 2, j % 2],
+            for bc in range(2):
+                nc.scalar.copy(
+                    out=sorted_sb[:, bc].rearrange("p u (wr a) -> p u wr a", a=8),
+                    in_=words[:, 0, bc],
                 )
+            nc.vector.tensor_copy(
+                out=sorted_sb[:, 2:4].rearrange("p bc u (wr a) -> p bc u wr a", a=8),
+                in_=words[:, 1],
+            )
             sorted_tiles[i] = sorted_sb
 
         def transpose_words(i):
@@ -152,10 +174,12 @@ def tile_switchnet_fstar_pa_t_e_kernel(tc, x, k1_words, k1_scales, b1, out):
                     in1=bias[:, :, 2 * br : 2 * br + 2, :],
                     op=mybir.AluOpType.add,
                 )
-            if s == TILES_PER_CHUNK - 1:
-                nc.sync.dma_start(out=out_chunks[c], in_=y_sb[:].rearrange("p s r j m -> p (s r j m)"))
+            if c == CHUNKS - 1:
+                nc.sync.dma_start(out=out_chunks[c][:, s, :], in_=y_sb[:, s].rearrange("p r j m -> p (r j m)"))
+            elif s == TILES_PER_CHUNK - 1:
+                nc.sync.dma_start(out=out_chunks[c], in_=y_sb[:].rearrange("p s r j m -> p s (r j m)"))
 
-        for t in range(TILES + 3):
+        def step(t):
             if t % TILES_PER_CHUNK == 0 and t // TILES_PER_CHUNK + LOADS_AHEAD < CHUNKS:
                 load(t // TILES_PER_CHUNK + LOADS_AHEAD)
             if 0 <= t - 2 < TILES:
@@ -168,3 +192,8 @@ def tile_switchnet_fstar_pa_t_e_kernel(tc, x, k1_words, k1_scales, b1, out):
                 multiply(t - 2)
             if 0 <= t - 3 < TILES:
                 add_bias(t - 3)
+
+        step(0)
+        spread_bias()
+        for t in range(1, TILES + 3):
+            step(t)

@@ -106,15 +106,13 @@ def tile_switchnet_fstar_pa_t_e_kernel(tc, x, k1_words, k1_scales, b1, out):
             words = x_tiles[c][:, s, :].bitcast(F32)
             words = words.rearrange("p (br wr bc a u) -> p br bc u wr a", br=2, wr=16, bc=2, a=8, u=2)
             sorted_sb = sorted_pool.tile([P, BLOCKS, 2, P], F32)
-            for bc in range(2):
-                nc.scalar.copy(
-                    out=sorted_sb[:, bc].rearrange("p u (wr a) -> p u wr a", a=8),
-                    in_=words[:, 0, bc],
+            scalar_blocks = 3 - i % 2
+            for j in range(BLOCKS):
+                copy = nc.scalar.copy if j < scalar_blocks else nc.vector.tensor_copy
+                copy(
+                    out=sorted_sb[:, j].rearrange("p u (wr a) -> p u wr a", a=8),
+                    in_=words[:, j // 2, j % 2],
                 )
-            nc.vector.tensor_copy(
-                out=sorted_sb[:, 2:4].rearrange("p bc u (wr a) -> p bc u wr a", a=8),
-                in_=words[:, 1],
-            )
             sorted_tiles[i] = sorted_sb
 
         def transpose_words(i):
@@ -193,7 +191,8 @@ def tile_switchnet_fstar_pa_t_e_kernel(tc, x, k1_words, k1_scales, b1, out):
             if 0 <= t - 3 < TILES:
                 add_bias(t - 3)
 
-        step(0)
+        for t in range(3):
+            step(t)
         spread_bias()
-        for t in range(1, TILES + 3):
+        for t in range(3, TILES + 3):
             step(t)

@@ -23,7 +23,7 @@ K_WORDS = K // 2
 TILES = SAMPLES // P
 TILES_PER_CHUNK = 2
 CHUNKS = TILES // TILES_PER_CHUNK
-LOADS_AHEAD = 6
+LOADS_AHEAD = 13
 
 FLOPS = 2 * SAMPLES * BLOCKS * K * L
 
@@ -39,7 +39,7 @@ def tile_switchnet_fstar_pa_t_e_kernel(tc, x, k1_words, k1_scales, b1, out):
         sorted_pool = stack.enter_context(tc.tile_pool(name="sorted", bufs=3))
         grouped_pool = stack.enter_context(tc.tile_pool(name="grouped", bufs=3))
         codes_pool = stack.enter_context(tc.tile_pool(name="codes", bufs=3))
-        y_pool = stack.enter_context(tc.tile_pool(name="y", bufs=4))
+        y_pool = stack.enter_context(tc.tile_pool(name="y", bufs=8))
         flipped_pool = stack.enter_context(tc.psum_pool(name="flipped", bufs=4))
         acc_pool = stack.enter_context(tc.psum_pool(name="acc", bufs=4))
         stack.enter_context(tc.manual_schedule())

@@ -19,6 +19,8 @@ R = 16
 M = 16
 WORDS = 1024
 K_WORDS = K // 2
+GRID_ROWS = 32
+SCALAR_ROWS = 20
 
 TILES = SAMPLES // P
 TILES_PER_CHUNK = 2
@@ -104,15 +106,10 @@ def tile_switchnet_fstar_pa_t_e_kernel(tc, x, k1_words, k1_scales, b1, out):
         def sort_words(i):
             c, s = divmod(i, TILES_PER_CHUNK)
             words = x_tiles[c][:, s, :].bitcast(F32)
-            words = words.rearrange("p (br wr bc a u) -> p br bc u wr a", br=2, wr=16, bc=2, a=8, u=2)
-            sorted_sb = sorted_pool.tile([P, BLOCKS, 2, P], F32)
-            scalar_blocks = 3 - i % 2
-            for j in range(BLOCKS):
-                copy = nc.scalar.copy if j < scalar_blocks else nc.vector.tensor_copy
-                copy(
-                    out=sorted_sb[:, j].rearrange("p u (wr a) -> p u wr a", a=8),
-                    in_=words[:, j // 2, j % 2],
-                )
+            words = words.rearrange("p (row bc a u) -> p bc u row a", row=GRID_ROWS, bc=2, a=8, u=2)
+            sorted_sb = sorted_pool.tile([P, 2, 2, GRID_ROWS, 8], F32)
+            nc.scalar.copy(out=sorted_sb[:, :, :, :SCALAR_ROWS, :], in_=words[:, :, :, :SCALAR_ROWS, :])
+            nc.vector.tensor_copy(out=sorted_sb[:, :, :, SCALAR_ROWS:, :], in_=words[:, :, :, SCALAR_ROWS:, :])
             sorted_tiles[i] = sorted_sb
 
         def transpose_words(i):
@@ -122,7 +119,11 @@ def tile_switchnet_fstar_pa_t_e_kernel(tc, x, k1_words, k1_scales, b1, out):
                 flipped = flipped_pool.tile([P, 2, 2, P], F32)
                 for bc in range(2):
                     for u in range(2):
-                        nc.tensor.transpose(flipped[:, bc, u, :], sorted_sb[:, 2 * br + bc, u, :], identity[:])
+                        nc.tensor.transpose(
+                            flipped[:, bc, u, :],
+                            sorted_sb[:, bc, u, 16 * br : 16 * br + 16, :].rearrange("p wr a -> p (wr a)"),
+                            identity[:],
+                        )
                 nc.scalar.copy(
                     out=grouped[:, 2 * br : 2 * br + 2].bitcast(F32),
                     in_=flipped[:].rearrange("p bc u b -> p bc b u"),

@@ -23,9 +23,11 @@ GRID_ROWS = 32
 SCALAR_ROWS = 20
 
 TILES = SAMPLES // P
-TILES_PER_CHUNK = 2
+TILES_PER_CHUNK = 8
 CHUNKS = TILES // TILES_PER_CHUNK
-LOADS_AHEAD = 13
+X_BUFFERS = 3
+MAX_STORE_TILES = 4
+Y_BUFFERS = 5
 
 FLOPS = 2 * SAMPLES * BLOCKS * K * L
 
@@ -37,11 +39,11 @@ def tile_switchnet_fstar_pa_t_e_kernel(tc, x, k1_words, k1_scales, b1, out):
 
     with ExitStack() as stack:
         consts = stack.enter_context(tc.tile_pool(name="consts", bufs=1))
-        x_pool = stack.enter_context(tc.tile_pool(name="x", bufs=LOADS_AHEAD + 1))
+        x_pool = stack.enter_context(tc.tile_pool(name="x", bufs=X_BUFFERS))
         sorted_pool = stack.enter_context(tc.tile_pool(name="sorted", bufs=3))
         grouped_pool = stack.enter_context(tc.tile_pool(name="grouped", bufs=3))
         codes_pool = stack.enter_context(tc.tile_pool(name="codes", bufs=3))
-        y_pool = stack.enter_context(tc.tile_pool(name="y", bufs=8))
+        y_pool = stack.enter_context(tc.tile_pool(name="y", bufs=Y_BUFFERS))
         flipped_pool = stack.enter_context(tc.psum_pool(name="flipped", bufs=4))
         acc_pool = stack.enter_context(tc.psum_pool(name="acc", bufs=4))
         stack.enter_context(tc.manual_schedule())
@@ -53,18 +55,37 @@ def tile_switchnet_fstar_pa_t_e_kernel(tc, x, k1_words, k1_scales, b1, out):
         acc_tiles = {}
         y_tiles = {}
 
-        def load(c):
-            x_sb = x_pool.tile([P, TILES_PER_CHUNK, 2 * WORDS], BF16)
-            if c == 0:
-                for s in range(TILES_PER_CHUNK):
-                    nc.sync.dma_start(out=x_sb[:, s, :], in_=x_chunks[c][:, s, :])
-            else:
-                nc.sync.dma_start(out=x_sb[:], in_=x_chunks[c])
-            x_tiles[c] = x_sb
+        def power_of_two_up_to(limit):
+            size = 1
+            while 2 * size <= limit:
+                size *= 2
+            return size
+
+        load_pieces = []
+        first = 0
+        while first < TILES:
+            size = min(power_of_two_up_to(max(first // 2, 1)), TILES_PER_CHUNK)
+            load_pieces.append((first, size))
+            first += size
+        store_of = {}
+        first = 0
+        while first < TILES:
+            size = min(power_of_two_up_to(max((TILES - first) // 2, 1)), MAX_STORE_TILES)
+            for i in range(first, first + size):
+                store_of[i] = (first, size)
+            first += size
+
+        def load(first_tile, tiles):
+            c, s = divmod(first_tile, TILES_PER_CHUNK)
+            if s == 0:
+                x_sb = x_pool.tile([P, TILES_PER_CHUNK, 2 * WORDS], BF16)
+                x_tiles[c] = x_sb
+            nc.sync.dma_start(out=x_tiles[c][:, s : s + tiles, :], in_=x_chunks[c][:, s : s + tiles, :])
 
         w_scales = consts.tile([P, BLOCKS, L], U8, align_bytes=64)
         nc.vector.memset(w_scales[:].rearrange("p j l -> p (j l)").bitcast(I32), 0)
-        load(0)
+        for first_tile, tiles in load_pieces[:2]:
+            load(first_tile, tiles)
         w_words = consts.tile([P, BLOCKS, L], U32, align_bytes=64)
         nc.sync.dma_start(
             out=w_words[:].bitcast(I32),
@@ -75,8 +96,9 @@ def tile_switchnet_fstar_pa_t_e_kernel(tc, x, k1_words, k1_scales, b1, out):
                 out=w_scales[32 * quadrant : 32 * quadrant + 4].bitcast(I32),
                 in_=k1_scales[:, 4 * quadrant : 4 * quadrant + 4, :].rearrange("j q l -> q j l").bitcast(I32),
             )
-        for c in range(1, LOADS_AHEAD):
-            load(c)
+        for first_tile, tiles in load_pieces[2:]:
+            if first_tile // TILES_PER_CHUNK < X_BUFFERS:
+                load(first_tile, tiles)
 
         identity = consts.tile([P, P], F32)
         make_identity(nc, identity[:])
@@ -161,26 +183,29 @@ def tile_switchnet_fstar_pa_t_e_kernel(tc, x, k1_words, k1_scales, b1, out):
             acc_tiles[i] = banks
 
         def add_bias(i):
-            c, s = divmod(i, TILES_PER_CHUNK)
-            if s == 0:
-                y_new = y_pool.tile([P, TILES_PER_CHUNK, R, BLOCKS, M], F32)
-                y_tiles[c] = y_new
-            y_sb = y_tiles[c]
+            first_tile, tiles = store_of[i]
+            if i == first_tile:
+                y_new = y_pool.tile([P, MAX_STORE_TILES, R, BLOCKS, M], F32)
+                y_tiles[first_tile] = y_new
+            y_sb = y_tiles[first_tile]
             for br, acc in enumerate(acc_tiles[i]):
                 nc.vector.tensor_tensor(
-                    out=y_sb[:, s, :, 2 * br : 2 * br + 2, :],
+                    out=y_sb[:, i - first_tile, :, 2 * br : 2 * br + 2, :],
                     in0=acc[:].rearrange("p bc (m r) -> p r bc m", m=M, r=R),
                     in1=bias[:, :, 2 * br : 2 * br + 2, :],
                     op=mybir.AluOpType.add,
                 )
-            if c == CHUNKS - 1:
-                nc.sync.dma_start(out=out_chunks[c][:, s, :], in_=y_sb[:, s].rearrange("p r j m -> p (r j m)"))
-            elif s == TILES_PER_CHUNK - 1:
-                nc.sync.dma_start(out=out_chunks[c], in_=y_sb[:].rearrange("p s r j m -> p s (r j m)"))
+            if i == first_tile + tiles - 1:
+                c, s = divmod(first_tile, TILES_PER_CHUNK)
+                nc.sync.dma_start(
+                    out=out_chunks[c][:, s : s + tiles, :],
+                    in_=y_sb[:, :tiles].rearrange("p s r j m -> p s (r j m)"),
+                )
 
         def step(t):
-            if t % TILES_PER_CHUNK == 0 and t // TILES_PER_CHUNK + LOADS_AHEAD < CHUNKS:
-                load(t // TILES_PER_CHUNK + LOADS_AHEAD)
+            for first_tile, tiles in load_pieces:
+                if first_tile // TILES_PER_CHUNK >= X_BUFFERS and first_tile - first_tile % TILES_PER_CHUNK == t + (X_BUFFERS - 1) * TILES_PER_CHUNK:
+                    load(first_tile, tiles)
             if 0 <= t - 2 < TILES:
                 quantise(t - 2)
             if t < TILES:

@@ -20,14 +20,16 @@ M = 16
 WORDS = 1024
 K_WORDS = K // 2
 GRID_ROWS = 32
-SCALAR_ROWS = 20
+SCALAR_ROWS = 23
 
 TILES = SAMPLES // P
 TILES_PER_CHUNK = 8
 CHUNKS = TILES // TILES_PER_CHUNK
 X_BUFFERS = 3
 MAX_STORE_TILES = 4
-Y_BUFFERS = 5
+SHORT_STORE_TILES = 2
+LAST_TILES = 12
+Y_BUFFERS = 6
 
 FLOPS = 2 * SAMPLES * BLOCKS * K * L
 
@@ -70,7 +72,12 @@ def tile_switchnet_fstar_pa_t_e_kernel(tc, x, k1_words, k1_scales, b1, out):
         store_of = {}
         first = 0
         while first < TILES:
-            size = min(power_of_two_up_to(max((TILES - first) // 2, 1)), MAX_STORE_TILES)
+            if TILES - first > LAST_TILES:
+                size = MAX_STORE_TILES
+            elif TILES - first > SHORT_STORE_TILES:
+                size = SHORT_STORE_TILES
+            else:
+                size = 1
             for i in range(first, first + size):
                 store_of[i] = (first, size)
             first += size

@@ -89,6 +89,10 @@ def tile_switchnet_fstar_pa_t_e_kernel(tc, x, k1_words, k1_scales, b1, out):
                 x_tiles[c] = x_sb
             nc.sync.dma_start(out=x_tiles[c][:, s : s + tiles, :], in_=x_chunks[c][:, s : s + tiles, :])
 
+        table_in = consts.tile([P, 1], F32)
+        nc.vector.memset(table_in[:], 0.0)
+        table_out = consts.tile([P, 1], F32)
+        nc.scalar.copy(out=table_out[:], in_=table_in[:])
         w_scales = consts.tile([P, BLOCKS, L], U8, align_bytes=64)
         nc.vector.memset(w_scales[:].rearrange("p j l -> p (j l)").bitcast(I32), 0)
         for first_tile, tiles in load_pieces[:2]:

@@ -21,6 +21,8 @@ WORDS = 1024
 K_WORDS = K // 2
 GRID_ROWS = 32
 SCALAR_ROWS = 23
+FIRST_SCALAR_ROWS = 12
+FIRST_TILES = 2
 
 TILES = SAMPLES // P
 TILES_PER_CHUNK = 8
@@ -141,8 +143,9 @@ def tile_switchnet_fstar_pa_t_e_kernel(tc, x, k1_words, k1_scales, b1, out):
             words = x_tiles[c][:, s, :].bitcast(F32)
             words = words.rearrange("p (row bc a u) -> p bc u row a", row=GRID_ROWS, bc=2, a=8, u=2)
             sorted_sb = sorted_pool.tile([P, 2, 2, GRID_ROWS, 8], F32)
-            nc.scalar.copy(out=sorted_sb[:, :, :, :SCALAR_ROWS, :], in_=words[:, :, :, :SCALAR_ROWS, :])
-            nc.vector.tensor_copy(out=sorted_sb[:, :, :, SCALAR_ROWS:, :], in_=words[:, :, :, SCALAR_ROWS:, :])
+            cut = FIRST_SCALAR_ROWS if i < FIRST_TILES else SCALAR_ROWS
+            nc.scalar.copy(out=sorted_sb[:, :, :, :cut, :], in_=words[:, :, :, :cut, :])
+            nc.vector.tensor_copy(out=sorted_sb[:, :, :, cut:, :], in_=words[:, :, :, cut:, :])
             sorted_tiles[i] = sorted_sb
 
         def transpose_words(i):
@@ -157,7 +160,8 @@ def tile_switchnet_fstar_pa_t_e_kernel(tc, x, k1_words, k1_scales, b1, out):
                             sorted_sb[:, bc, u, 16 * br : 16 * br + 16, :].rearrange("p wr a -> p (wr a)"),
                             identity[:],
                         )
-                nc.scalar.copy(
+                copy_out = nc.vector.tensor_copy if i == 0 and br == 1 else nc.scalar.copy
+                copy_out(
                     out=grouped[:, 2 * br : 2 * br + 2].bitcast(F32),
                     in_=flipped[:].rearrange("p bc u b -> p bc b u"),
                 )
@@ -217,19 +221,22 @@ def tile_switchnet_fstar_pa_t_e_kernel(tc, x, k1_words, k1_scales, b1, out):
             for first_tile, tiles in load_pieces:
                 if first_tile // TILES_PER_CHUNK >= X_BUFFERS and first_tile - first_tile % TILES_PER_CHUNK == t + (X_BUFFERS - 1) * TILES_PER_CHUNK:
                     load(first_tile, tiles)
-            if 0 <= t - 2 < TILES:
+            quantise_ahead = 0 <= t - 2 < TILES
+            if quantise_ahead:
                 quantise(t - 2)
+            if t == 2:
+                spread_bias()
             if t < TILES:
                 sort_words(t)
             if 0 <= t - 1 < TILES:
                 transpose_words(t - 1)
-            if 0 <= t - 2 < TILES:
+            if quantise_ahead:
                 multiply(t - 2)
             if 0 <= t - 3 < TILES:
                 add_bias(t - 3)
 
-        for t in range(3):
-            step(t)
-        spread_bias()
-        for t in range(3, TILES + 3):
+        sort_words(0)
+        transpose_words(0)
+        sort_words(1)
+        for t in range(2, TILES + 3):
             step(t)

@@ -20,7 +20,7 @@ M = 16
 WORDS = 1024
 K_WORDS = K // 2
 GRID_ROWS = 32
-SCALAR_ROWS = 23
+SCALAR_ROWS = 21
 FIRST_SCALAR_ROWS = 12
 FIRST_TILES = 2
 

@@ -28,10 +28,8 @@ TILES = SAMPLES // P
 TILES_PER_CHUNK = 8
 CHUNKS = TILES // TILES_PER_CHUNK
 X_BUFFERS = 3
-MAX_STORE_TILES = 4
-SHORT_STORE_TILES = 2
-LAST_TILES = 12
-Y_BUFFERS = 6
+STORE_TILES = (8, 8, 4, 4, 2, 2, 2, 1, 1)
+Y_BUFFERS = 3
 
 FLOPS = 2 * SAMPLES * BLOCKS * K * L
 
@@ -65,21 +63,15 @@ def tile_switchnet_fstar_pa_t_e_kernel(tc, x, k1_words, k1_scales, b1, out):
                 size *= 2
             return size
 
-        load_pieces = []
-        first = 0
+        load_pieces = [(0, 1), (1, 1), (2, 2)]
+        first = 4
         while first < TILES:
-            size = min(power_of_two_up_to(max(first // 2, 1)), TILES_PER_CHUNK)
+            size = min(power_of_two_up_to(first // 2), TILES_PER_CHUNK)
             load_pieces.append((first, size))
             first += size
         store_of = {}
         first = 0
-        while first < TILES:
-            if TILES - first > LAST_TILES:
-                size = MAX_STORE_TILES
-            elif TILES - first > SHORT_STORE_TILES:
-                size = SHORT_STORE_TILES
-            else:
-                size = 1
+        for size in STORE_TILES:
             for i in range(first, first + size):
                 store_of[i] = (first, size)
             first += size
@@ -198,23 +190,24 @@ def tile_switchnet_fstar_pa_t_e_kernel(tc, x, k1_words, k1_scales, b1, out):
             acc_tiles[i] = banks
 
         def add_bias(i):
-            first_tile, tiles = store_of[i]
-            if i == first_tile:
-                y_new = y_pool.tile([P, MAX_STORE_TILES, R, BLOCKS, M], F32)
-                y_tiles[first_tile] = y_new
-            y_sb = y_tiles[first_tile]
+            c, s = divmod(i, TILES_PER_CHUNK)
+            if s == 0:
+                y_new = y_pool.tile([P, TILES_PER_CHUNK, R, BLOCKS, M], F32)
+                y_tiles[c] = y_new
+            y_sb = y_tiles[c]
             for br, acc in enumerate(acc_tiles[i]):
                 nc.vector.tensor_tensor(
-                    out=y_sb[:, i - first_tile, :, 2 * br : 2 * br + 2, :],
+                    out=y_sb[:, s, :, 2 * br : 2 * br + 2, :],
                     in0=acc[:].rearrange("p bc (m r) -> p r bc m", m=M, r=R),
                     in1=bias[:, :, 2 * br : 2 * br + 2, :],
                     op=mybir.AluOpType.add,
                 )
+            first_tile, tiles = store_of[i]
             if i == first_tile + tiles - 1:
-                c, s = divmod(first_tile, TILES_PER_CHUNK)
+                s = first_tile % TILES_PER_CHUNK
                 nc.sync.dma_start(
                     out=out_chunks[c][:, s : s + tiles, :],
-                    in_=y_sb[:, :tiles].rearrange("p s r j m -> p s (r j m)"),
+                    in_=y_sb[:, s : s + tiles].rearrange("p s r j m -> p s (r j m)"),
                 )
 
         def step(t):

@@ -29,6 +29,7 @@ TILES_PER_CHUNK = 8
 CHUNKS = TILES // TILES_PER_CHUNK
 X_BUFFERS = 3
 STORE_TILES = (8, 8, 4, 4, 2, 2, 2, 1, 1)
+DMA_ALIGN = 256
 Y_BUFFERS = 3
 
 FLOPS = 2 * SAMPLES * BLOCKS * K * L
@@ -63,10 +64,10 @@ def tile_switchnet_fstar_pa_t_e_kernel(tc, x, k1_words, k1_scales, b1, out):
                 size *= 2
             return size
 
-        load_pieces = [(0, 1), (1, 1), (2, 2)]
-        first = 4
+        load_pieces = []
+        first = 0
         while first < TILES:
-            size = min(power_of_two_up_to(first // 2), TILES_PER_CHUNK)
+            size = min(power_of_two_up_to(max(first // 2, 1)), TILES_PER_CHUNK)
             load_pieces.append((first, size))
             first += size
         store_of = {}
@@ -79,7 +80,7 @@ def tile_switchnet_fstar_pa_t_e_kernel(tc, x, k1_words, k1_scales, b1, out):
         def load(first_tile, tiles):
             c, s = divmod(first_tile, TILES_PER_CHUNK)
             if s == 0:
-                x_sb = x_pool.tile([P, TILES_PER_CHUNK, 2 * WORDS], BF16)
+                x_sb = x_pool.tile([P, TILES_PER_CHUNK, 2 * WORDS], BF16, align_bytes=DMA_ALIGN)
                 x_tiles[c] = x_sb
             nc.sync.dma_start(out=x_tiles[c][:, s : s + tiles, :], in_=x_chunks[c][:, s : s + tiles, :])
 
@@ -192,7 +193,7 @@ def tile_switchnet_fstar_pa_t_e_kernel(tc, x, k1_words, k1_scales, b1, out):
         def add_bias(i):
             c, s = divmod(i, TILES_PER_CHUNK)
             if s == 0:
-                y_new = y_pool.tile([P, TILES_PER_CHUNK, R, BLOCKS, M], F32)
+                y_new = y_pool.tile([P, TILES_PER_CHUNK, R, BLOCKS, M], F32, align_bytes=DMA_ALIGN)
                 y_tiles[c] = y_new
             y_sb = y_tiles[c]
             for br, acc in enumerate(acc_tiles[i]):

from contextlib import ExitStack

import concourse.mybir as mybir
from concourse.masks import make_identity

F32 = mybir.dt.float32
BF16 = mybir.dt.bfloat16
I32 = mybir.dt.int32
U32 = mybir.dt.uint32
U8 = mybir.dt.uint8
FP8X4 = mybir.dt.float8_e4m3fn_x4

P = 128
SAMPLES = 4096
BLOCKS = 4
K = 512
L = 256
R = 16
M = 16
WORDS = 1024
K_WORDS = K // 2
GRID_ROWS = 32
SCALAR_ROWS = 21
FIRST_SCALAR_ROWS = 12
FIRST_TILES = 2

TILES = SAMPLES // P
TILES_PER_CHUNK = 8
CHUNKS = TILES // TILES_PER_CHUNK
X_BUFFERS = 3
STORE_TILES = (8, 8, 4, 4, 2, 2, 2, 1, 1)
DMA_ALIGN = 256
Y_BUFFERS = 3

FLOPS = 2 * SAMPLES * BLOCKS * K * L


def tile_switchnet_fstar_pa_t_e_kernel(tc, x, k1_words, k1_scales, b1, out):
    nc = tc.nc
    x_chunks = x.rearrange("(c p s) g ch -> c p s (g ch)", p=P, s=TILES_PER_CHUNK)
    out_chunks = out.rearrange("(c p s) q r -> c p s (q r)", p=P, s=TILES_PER_CHUNK)

    with ExitStack() as stack:
        consts = stack.enter_context(tc.tile_pool(name="consts", bufs=1))
        x_pool = stack.enter_context(tc.tile_pool(name="x", bufs=X_BUFFERS))
        sorted_pool = stack.enter_context(tc.tile_pool(name="sorted", bufs=3))
        grouped_pool = stack.enter_context(tc.tile_pool(name="grouped", bufs=3))
        codes_pool = stack.enter_context(tc.tile_pool(name="codes", bufs=3))
        y_pool = stack.enter_context(tc.tile_pool(name="y", bufs=Y_BUFFERS))
        flipped_pool = stack.enter_context(tc.psum_pool(name="flipped", bufs=4))
        acc_pool = stack.enter_context(tc.psum_pool(name="acc", bufs=4))
        stack.enter_context(tc.manual_schedule())

        x_tiles = {}
        sorted_tiles = {}
        grouped_tiles = {}
        codes_tiles = {}
        acc_tiles = {}
        y_tiles = {}

        def power_of_two_up_to(limit):
            size = 1
            while 2 * size <= limit:
                size *= 2
            return size

        load_pieces = []
        first = 0
        while first < TILES:
            size = min(power_of_two_up_to(max(first // 2, 1)), TILES_PER_CHUNK)
            load_pieces.append((first, size))
            first += size
        store_of = {}
        first = 0
        for size in STORE_TILES:
            for i in range(first, first + size):
                store_of[i] = (first, size)
            first += size

        def load(first_tile, tiles):
            c, s = divmod(first_tile, TILES_PER_CHUNK)
            if s == 0:
                x_sb = x_pool.tile([P, TILES_PER_CHUNK, 2 * WORDS], BF16, align_bytes=DMA_ALIGN)
                x_tiles[c] = x_sb
            nc.sync.dma_start(out=x_tiles[c][:, s : s + tiles, :], in_=x_chunks[c][:, s : s + tiles, :])

        table_in = consts.tile([P, 1], F32)
        nc.vector.memset(table_in[:], 0.0)
        table_out = consts.tile([P, 1], F32)
        nc.scalar.copy(out=table_out[:], in_=table_in[:])
        w_scales = consts.tile([P, BLOCKS, L], U8, align_bytes=64)
        nc.vector.memset(w_scales[:].rearrange("p j l -> p (j l)").bitcast(I32), 0)
        for first_tile, tiles in load_pieces[:2]:
            load(first_tile, tiles)
        w_words = consts.tile([P, BLOCKS, L], U32, align_bytes=64)
        nc.sync.dma_start(
            out=w_words[:].bitcast(I32),
            in_=k1_words.rearrange("j p l t -> p j (l t)").bitcast(I32),
        )
        for quadrant in range(4):
            nc.sync.dma_start(
                out=w_scales[32 * quadrant : 32 * quadrant + 4].bitcast(I32),
                in_=k1_scales[:, 4 * quadrant : 4 * quadrant + 4, :].rearrange("j q l -> q j l").bitcast(I32),
            )
        for first_tile, tiles in load_pieces[2:]:
            if first_tile // TILES_PER_CHUNK < X_BUFFERS:
                load(first_tile, tiles)

        identity = consts.tile([P, P], F32)
        make_identity(nc, identity[:])

        ones = consts.tile([P, P], BF16)
        nc.vector.memset(ones[:], 1.0)
        bias_row = consts.tile([P, BLOCKS, L], BF16)
        nc.vector.memset(bias_row[:], 0.0)
        nc.scalar.dma_start(out=bias_row[0:1], in_=b1)
        bias = consts.tile([P, R, BLOCKS, M], F32)

        def spread_bias():
            for br in range(2):
                spread = acc_pool.tile([P, 2, L], F32, tag="acc")
                nc.tensor.matmul(
                    out=spread[:].rearrange("p bc l -> p (bc l)"),
                    lhsT=ones[:],
                    rhs=bias_row[:, 2 * br : 2 * br + 2, :].rearrange("p bc l -> p (bc l)"),
                    start=True,
                    stop=True,
                )
                nc.vector.tensor_copy(
                    out=bias[:, :, 2 * br : 2 * br + 2, :],
                    in_=spread[:].rearrange("p bc (m r) -> p r bc m", m=M, r=R),
                )

        def sort_words(i):
            c, s = divmod(i, TILES_PER_CHUNK)
            words = x_tiles[c][:, s, :].bitcast(F32)
            words = words.rearrange("p (row bc a u) -> p bc u row a", row=GRID_ROWS, bc=2, a=8, u=2)
            sorted_sb = sorted_pool.tile([P, 2, 2, GRID_ROWS, 8], F32)
            cut = FIRST_SCALAR_ROWS if i < FIRST_TILES else SCALAR_ROWS
            nc.scalar.copy(out=sorted_sb[:, :, :, :cut, :], in_=words[:, :, :, :cut, :])
            nc.vector.tensor_copy(out=sorted_sb[:, :, :, cut:, :], in_=words[:, :, :, cut:, :])
            sorted_tiles[i] = sorted_sb

        def transpose_words(i):
            sorted_sb = sorted_tiles[i]
            grouped = grouped_pool.tile([P, BLOCKS, P, 4], BF16, align_bytes=64)
            for br in range(2):
                flipped = flipped_pool.tile([P, 2, 2, P], F32)
                for bc in range(2):
                    for u in range(2):
                        nc.tensor.transpose(
                            flipped[:, bc, u, :],
                            sorted_sb[:, bc, u, 16 * br : 16 * br + 16, :].rearrange("p wr a -> p (wr a)"),
                            identity[:],
                        )
                copy_out = nc.vector.tensor_copy if i == 0 and br == 1 else nc.scalar.copy
                copy_out(
                    out=grouped[:, 2 * br : 2 * br + 2].bitcast(F32),
                    in_=flipped[:].rearrange("p bc u b -> p bc b u"),
                )
            grouped_tiles[i] = grouped

        def quantise(i):
            grouped = grouped_tiles[i]
            codes = codes_pool.tile([P, BLOCKS, P], U32, align_bytes=64)
            scales = codes_pool.tile([P, BLOCKS, P], U8, align_bytes=64)
            nc.vector.quantize_mx(
                out=codes[:].rearrange("p j b -> p (j b)").bitcast(FP8X4),
                scales=scales[:].rearrange("p j b -> p (j b)"),
                in_=grouped[:].rearrange("p j b t -> p (j b t)"),
            )
            codes_tiles[i] = (codes, scales)

        def multiply(i):
            codes, scales = codes_tiles[i]
            banks = []
            for br in range(2):
                acc = acc_pool.tile([P, 2, L], F32)
                for bc in range(2):
                    j = 2 * br + bc
                    nc.tensor.matmul_mx(
                        out=acc[:, bc, :],
                        lhsT=codes[:, j, :].bitcast(FP8X4),
                        lhsT_scale=scales[:, j, :],
                        rhs=w_words[:, j, :].bitcast(FP8X4),
                        rhs_scale=w_scales[:, j, :],
                        start=True,
                        stop=True,
                    )
                banks.append(acc)
            acc_tiles[i] = banks

        def add_bias(i):
            c, s = divmod(i, TILES_PER_CHUNK)
            if s == 0:
                y_new = y_pool.tile([P, TILES_PER_CHUNK, R, BLOCKS, M], F32, align_bytes=DMA_ALIGN)
                y_tiles[c] = y_new
            y_sb = y_tiles[c]
            for br, acc in enumerate(acc_tiles[i]):
                nc.vector.tensor_tensor(
                    out=y_sb[:, s, :, 2 * br : 2 * br + 2, :],
                    in0=acc[:].rearrange("p bc (m r) -> p r bc m", m=M, r=R),
                    in1=bias[:, :, 2 * br : 2 * br + 2, :],
                    op=mybir.AluOpType.add,
                )
            first_tile, tiles = store_of[i]
            if i == first_tile + tiles - 1:
                s = first_tile % TILES_PER_CHUNK
                nc.sync.dma_start(
                    out=out_chunks[c][:, s : s + tiles, :],
                    in_=y_sb[:, s : s + tiles].rearrange("p s r j m -> p s (r j m)"),
                )

        def step(t):
            for first_tile, tiles in load_pieces:
                if first_tile // TILES_PER_CHUNK >= X_BUFFERS and first_tile - first_tile % TILES_PER_CHUNK == t + (X_BUFFERS - 1) * TILES_PER_CHUNK:
                    load(first_tile, tiles)
            quantise_ahead = 0 <= t - 2 < TILES
            if quantise_ahead:
                quantise(t - 2)
            if t == 2:
                spread_bias()
            if t < TILES:
                sort_words(t)
            if 0 <= t - 1 < TILES:
                transpose_words(t - 1)
            if quantise_ahead:
                multiply(t - 2)
            if 0 <= t - 3 < TILES:
                add_bias(t - 3)

        sort_words(0)
        transpose_words(0)
        sort_words(1)
        for t in range(2, TILES + 3):
            step(t)
